import numpy as np
import ml_dtypes

BF16 = ml_dtypes.bfloat16


def bf(x):
    return np.asarray(x, np.float32).astype(BF16)


def f32(x):
    return np.asarray(x, np.float32)


def f64(x):
    return np.asarray(x).astype(np.float64)


def striped(idx):
    return np.tile(idx.reshape(-1, 16).T, (8, 1))


C, S, K, H, R, N, O1, O2 = 128, 1024, 4, 512, 8, 4096, 256, 2048
NEG_SLOPE = 0.2


def leaky(v):
    return np.maximum(v, NEG_SLOPE * v)


def setup_inputs():
    return {
        "x": bf(np.random.standard_normal((C, S))),
        "w1n": bf(np.random.standard_normal((C, O1)) / np.sqrt(2.0 * C)),
        "w1c": bf(np.random.standard_normal((C, O1)) / np.sqrt(2.0 * C)),
        "b1": f32(0.1 * np.random.standard_normal((O1, 1))),
        "w2n": bf(np.random.standard_normal((O1, O2)) / np.sqrt(2.0 * O1)),
        "w2c": bf(np.random.standard_normal((O1, O2)) / np.sqrt(2.0 * O1)),
        "b2": f32(0.1 * np.random.standard_normal((O2, 1))),
        "offs": striped(np.concatenate([np.random.permutation(S)[:H] for _ in range(R)])),
    }


def reference(x, w1n, w1c, b1, w2n, w2c, b2, offs):
    idx = offs[:16].T.reshape(-1)
    x, w1n, w1c, b1 = f64(x), f64(w1n), f64(w1c), f64(b1)
    w2n, w2c, b2 = f64(w2n), f64(w2c), f64(b2)
    near = (w1n.T @ x[:, idx]).reshape(O1, K, S)
    own = w1c.T @ x - w1n.T @ x + b1
    x1 = leaky(near + own[:, None, :]).max(axis=1)
    u2 = w2n.T @ x1
    t2 = w2c.T @ x1 - u2 + b2
    return np.concatenate([x1, u2, t2], axis=0)

@@ -1,0 +1,124 @@
+import concourse.mybir as mybir
+from concourse.masks import make_identity
+
+BF16, F32, U16 = mybir.dt.bfloat16, mybir.dt.float32, mybir.dt.uint16
+ALU = mybir.AluOpType
+ACT = mybir.ActivationFunctionType
+
+P = 128
+NODES = 1024
+NEIGHBOURS = 4
+BANK = 512
+HALVES = NODES // BANK
+F1_BLOCKS = 2
+F2_BLOCKS = 16
+GROUP = 2
+NEG_SLOPE = 0.2
+
+FLOPS = 2 * P * 256 * (NEIGHBOURS * NODES) + 2 * 2 * P * 256 * NODES + 2 * 2 * 256 * 2048 * NODES
+
+
+def tile_skeletonconv_b_kernel(tc, x, w1n, w1c, b1, w2n, w2c, b2, offs, out):
+    nc = tc.nc
+    with (
+        tc.tile_pool(name="held", bufs=1) as held,
+        tc.tile_pool(name="work", bufs=3) as work,
+        tc.tile_pool(name="stage", bufs=6) as stage,
+        tc.psum_pool(name="psum", bufs=8) as psum,
+    ):
+        offsets = held.tile([P, NEIGHBOURS * NODES // 16], U16, name="offsets")
+        nc.sync.dma_start(offsets[:], offs)
+        x_sb = held.tile([P, NODES], BF16, name="x_sb")
+        nc.sync.dma_start(x_sb[:], x)
+        w1n_sb = held.tile([P, F1_BLOCKS * P], BF16, name="w1n_sb")
+        nc.scalar.dma_start(w1n_sb[:], w1n)
+        w1c_sb = held.tile([P, F1_BLOCKS * P], BF16, name="w1c_sb")
+        nc.scalar.dma_start(w1c_sb[:], w1c)
+
+        bias_rows = held.tile([P, P], F32, name="bias_rows")
+        nc.vector.memset(bias_rows[:], 0.0)
+        nc.scalar.dma_start(bias_rows[0:F2_BLOCKS, :], b2.rearrange("(q p) o -> q (p o)", p=P))
+        nc.scalar.dma_start(
+            bias_rows[F2_BLOCKS : F2_BLOCKS + F1_BLOCKS, :], b1.rearrange("(m p) o -> m (p o)", p=P)
+        )
+
+        w2n_sb = held.tile([P, F1_BLOCKS, F2_BLOCKS * P], BF16, name="w2n_sb")
+        nc.sync.dma_start(w2n_sb[:], w2n.rearrange("(k p) q -> p k q", p=P))
+        w2c_sb = held.tile([P, F1_BLOCKS, F2_BLOCKS * P], BF16, name="w2c_sb")
+        nc.scalar.dma_start(w2c_sb[:], w2c.rearrange("(k p) q -> p k q", p=P))
+
+        identity = held.tile([P, P], F32, name="identity")
+        make_identity(nc, identity[:])
+        bias_bank = psum.tile([P, BANK], F32, name="bias_bank", tag="bank")
+        nc.tensor.transpose(bias_bank[:, 0:P], bias_rows[:], identity[:])
+        bias_cols = held.tile([P, F2_BLOCKS + F1_BLOCKS], F32, name="bias_cols")
+        nc.vector.tensor_copy(bias_cols[:], bias_bank[:, 0 : F2_BLOCKS + F1_BLOCKS])
+
+        w1n_neg = held.tile([P, F1_BLOCKS * P], BF16, name="w1n_neg")
+        nc.vector.tensor_scalar_mul(w1n_neg[:], w1n_sb[:], -1.0)
+
+        own = [held.tile([P, NODES], F32, name=f"own{m}") for m in range(F1_BLOCKS)]
+        for c in range(HALVES):
+            half = slice(c * BANK, (c + 1) * BANK)
+            for m in range(F1_BLOCKS):
+                block = slice(m * P, (m + 1) * P)
+                own_bank = psum.tile([P, BANK], F32, name="own_bank", tag="bank")
+                nc.tensor.matmul(own_bank[:], w1c_sb[:, block], x_sb[:, half], start=True, stop=False)
+                nc.tensor.matmul(own_bank[:], w1n_neg[:, block], x_sb[:, half], start=False, stop=True)
+                b1_col = bias_cols[:, F2_BLOCKS + m : F2_BLOCKS + m + 1]
+                nc.scalar.activation(own[m][:, half], own_bank[:], ACT.Identity, bias=b1_col)
+
+        x1_f32 = [held.tile([P, NODES], F32, name=f"x1_f32_{m}") for m in range(F1_BLOCKS)]
+        x1_bf = [held.tile([P, NODES], BF16, name=f"x1_bf_{m}") for m in range(F1_BLOCKS)]
+        for c in range(HALVES):
+            half = slice(c * BANK, (c + 1) * BANK)
+            for m in range(F1_BLOCKS):
+                block = slice(m * P, (m + 1) * P)
+                near = [psum.tile([P, BANK], F32, name=f"near{r}", tag="bank") for r in range(NEIGHBOURS)]
+                for r in range(NEIGHBOURS):
+                    piece = r * HALVES + c
+                    piece_offsets = offsets[:, piece * (BANK // 16) : (piece + 1) * (BANK // 16)]
+                    nc.tensor.matmul(
+                        near[r][:], w1n_sb[:, block], x_sb[:].indirect(piece_offsets), start=True, stop=True
+                    )
+                best = work.tile([P, BANK], F32, name="best")
+                nc.scalar.copy(best[:], near[0][:])
+                for r in range(1, NEIGHBOURS):
+                    nc.vector.tensor_max(best[:], near[r][:], best[:])
+                nc.vector.tensor_add(best[:], best[:], own[m][:, half])
+                nc.vector.scalar_tensor_tensor(
+                    out=x1_f32[m][:, half], in0=best[:], scalar=NEG_SLOPE, in1=best[:], op0=ALU.mult, op1=ALU.max
+                )
+                nc.scalar.copy(x1_bf[m][:, half], x1_f32[m][:, half])
+                nc.sync.dma_start(out[block, half], x1_f32[m][:, half])
+
+        u2_rows = out[F1_BLOCKS * P : (F1_BLOCKS + F2_BLOCKS) * P, :].rearrange("(q p) n -> p q n", p=P)
+        t2_rows = out[(F1_BLOCKS + F2_BLOCKS) * P :, :].rearrange("(q p) n -> p q n", p=P)
+        for c in range(HALVES):
+            half = slice(c * BANK, (c + 1) * BANK)
+            for g in range(F2_BLOCKS // GROUP):
+                u2_sb = stage.tile([P, GROUP, BANK], F32, name="u2_sb")
+                t2_sb = stage.tile([P, GROUP, BANK], F32, name="t2_sb")
+                for i in range(GROUP):
+                    q = g * GROUP + i
+                    block = slice(q * P, (q + 1) * P)
+                    u2_bank = psum.tile([P, BANK], F32, name="u2_bank", tag="bank")
+                    c2_bank = psum.tile([P, BANK], F32, name="c2_bank", tag="bank")
+                    for k in range(F1_BLOCKS):
+                        first, last = k == 0, k == F1_BLOCKS - 1
+                        nc.tensor.matmul(u2_bank[:], w2n_sb[:, k, block], x1_bf[k][:, half], start=first, stop=last)
+                    for k in range(F1_BLOCKS):
+                        first, last = k == 0, k == F1_BLOCKS - 1
+                        nc.tensor.matmul(c2_bank[:], w2c_sb[:, k, block], x1_bf[k][:, half], start=first, stop=last)
+                    nc.scalar.copy(u2_sb[:, i, :], u2_bank[:])
+                    nc.vector.scalar_tensor_tensor(
+                        out=t2_sb[:, i, :],
+                        in0=c2_bank[:],
+                        scalar=bias_cols[:, q : q + 1],
+                        in1=u2_sb[:, i, :],
+                        op0=ALU.add,
+                        op1=ALU.subtract,
+                    )
+                group = slice(g * GROUP, (g + 1) * GROUP)
+                nc.sync.dma_start(u2_rows[:, group, half], u2_sb[:])
+                nc.sync.dma_start(t2_rows[:, group, half], t2_sb[:])

@@ -1,5 +1,4 @@
 import concourse.mybir as mybir
-from concourse.masks import make_identity
 
 BF16, F32, U16 = mybir.dt.bfloat16, mybir.dt.float32, mybir.dt.uint16
 ALU = mybir.AluOpType
@@ -10,8 +9,8 @@ NODES = 1024
 NEIGHBOURS = 4
 BANK = 512
 HALVES = NODES // BANK
-F1_BLOCKS = 2
-F2_BLOCKS = 16
+B1 = 2
+B2 = 16
 GROUP = 2
 NEG_SLOPE = 0.2
 
@@ -23,102 +22,96 @@ def tile_skeletonconv_b_kernel(tc, x, w1n, w1c, b1, w2n, w2c, b2, offs, out):
     with (
         tc.tile_pool(name="held", bufs=1) as held,
         tc.tile_pool(name="work", bufs=3) as work,
-        tc.tile_pool(name="stage", bufs=6) as stage,
+        tc.tile_pool(name="stage", bufs=4) as stage,
         tc.psum_pool(name="psum", bufs=8) as psum,
     ):
         offsets = held.tile([P, NEIGHBOURS * NODES // 16], U16, name="offsets")
         nc.sync.dma_start(offsets[:], offs)
         x_sb = held.tile([P, NODES], BF16, name="x_sb")
-        nc.sync.dma_start(x_sb[:], x)
-        w1n_sb = held.tile([P, F1_BLOCKS * P], BF16, name="w1n_sb")
-        nc.scalar.dma_start(w1n_sb[:], w1n)
-        w1c_sb = held.tile([P, F1_BLOCKS * P], BF16, name="w1c_sb")
-        nc.scalar.dma_start(w1c_sb[:], w1c)
+        nc.scalar.dma_start(x_sb[:], x)
+        w1n_sb = held.tile([P, B1 * P], BF16, name="w1n_sb")
+        nc.sync.dma_start(w1n_sb[:], w1n)
+        w1c_sb = held.tile([P, B1 * P], BF16, name="w1c_sb")
+        nc.sync.dma_start(w1c_sb[:], w1c)
+        b1_cols = held.tile([P, B1], F32, name="b1_cols")
+        nc.scalar.dma_start(b1_cols[:], b1.rearrange("(p i) o -> p (i o)", i=B1))
+        b2_cols = held.tile([P, B2], F32, name="b2_cols")
+        nc.scalar.dma_start(b2_cols[:], b2.rearrange("(p i) o -> p (i o)", i=B2))
+        w2n_sb = held.tile([P, B1, B2 * P], BF16, name="w2n_sb")
+        nc.sync.dma_start(w2n_sb[:], w2n.rearrange("(p k) q -> p k q", k=B1))
+        w2c_sb = held.tile([P, B1, B2 * P], BF16, name="w2c_sb")
+        nc.scalar.dma_start(w2c_sb[:], w2c.rearrange("(p k) q -> p k q", k=B1))
 
-        bias_rows = held.tile([P, P], F32, name="bias_rows")
-        nc.vector.memset(bias_rows[:], 0.0)
-        nc.scalar.dma_start(bias_rows[0:F2_BLOCKS, :], b2.rearrange("(q p) o -> q (p o)", p=P))
-        nc.scalar.dma_start(
-            bias_rows[F2_BLOCKS : F2_BLOCKS + F1_BLOCKS, :], b1.rearrange("(m p) o -> m (p o)", p=P)
-        )
+        w1n_blocks = held.tile([P, B1, P], BF16, name="w1n_blocks")
+        nc.vector.tensor_copy(w1n_blocks[:], w1n_sb[:].rearrange("p (j i) -> p i j", i=B1))
+        w1n_neg_blocks = held.tile([P, B1, P], BF16, name="w1n_neg_blocks")
+        nc.vector.tensor_scalar_mul(w1n_neg_blocks[:], w1n_sb[:].rearrange("p (j i) -> p i j", i=B1), -1.0)
+        w1c_blocks = held.tile([P, B1, P], BF16, name="w1c_blocks")
+        nc.vector.tensor_copy(w1c_blocks[:], w1c_sb[:].rearrange("p (j i) -> p i j", i=B1))
 
-        w2n_sb = held.tile([P, F1_BLOCKS, F2_BLOCKS * P], BF16, name="w2n_sb")
-        nc.sync.dma_start(w2n_sb[:], w2n.rearrange("(k p) q -> p k q", p=P))
-        w2c_sb = held.tile([P, F1_BLOCKS, F2_BLOCKS * P], BF16, name="w2c_sb")
-        nc.scalar.dma_start(w2c_sb[:], w2c.rearrange("(k p) q -> p k q", p=P))
-
-        identity = held.tile([P, P], F32, name="identity")
-        make_identity(nc, identity[:])
-        bias_bank = psum.tile([P, BANK], F32, name="bias_bank", tag="bank")
-        nc.tensor.transpose(bias_bank[:, 0:P], bias_rows[:], identity[:])
-        bias_cols = held.tile([P, F2_BLOCKS + F1_BLOCKS], F32, name="bias_cols")
-        nc.vector.tensor_copy(bias_cols[:], bias_bank[:, 0 : F2_BLOCKS + F1_BLOCKS])
-
-        w1n_neg = held.tile([P, F1_BLOCKS * P], BF16, name="w1n_neg")
-        nc.vector.tensor_scalar_mul(w1n_neg[:], w1n_sb[:], -1.0)
-
-        own = [held.tile([P, NODES], F32, name=f"own{m}") for m in range(F1_BLOCKS)]
+        own = held.tile([P, B1, NODES], F32, name="own")
         for c in range(HALVES):
             half = slice(c * BANK, (c + 1) * BANK)
-            for m in range(F1_BLOCKS):
-                block = slice(m * P, (m + 1) * P)
+            for i in range(B1):
                 own_bank = psum.tile([P, BANK], F32, name="own_bank", tag="bank")
-                nc.tensor.matmul(own_bank[:], w1c_sb[:, block], x_sb[:, half], start=True, stop=False)
-                nc.tensor.matmul(own_bank[:], w1n_neg[:, block], x_sb[:, half], start=False, stop=True)
-                b1_col = bias_cols[:, F2_BLOCKS + m : F2_BLOCKS + m + 1]
-                nc.scalar.activation(own[m][:, half], own_bank[:], ACT.Identity, bias=b1_col)
+                nc.tensor.matmul(own_bank[:], w1c_blocks[:, i, :], x_sb[:, half], start=True, stop=False)
+                nc.tensor.matmul(own_bank[:], w1n_neg_blocks[:, i, :], x_sb[:, half], start=False, stop=True)
+                nc.scalar.activation(own[:, i, half], own_bank[:], ACT.Identity, bias=b1_cols[:, i : i + 1])
 
-        x1_f32 = [held.tile([P, NODES], F32, name=f"x1_f32_{m}") for m in range(F1_BLOCKS)]
-        x1_bf = [held.tile([P, NODES], BF16, name=f"x1_bf_{m}") for m in range(F1_BLOCKS)]
+        x1_rows = out[0 : B1 * P, :].rearrange("(p i) n -> p i n", i=B1)
+        x1_f32 = held.tile([P, B1, NODES], F32, name="x1_f32")
+        x1_bf = held.tile([P, B1, NODES], BF16, name="x1_bf")
         for c in range(HALVES):
             half = slice(c * BANK, (c + 1) * BANK)
-            for m in range(F1_BLOCKS):
-                block = slice(m * P, (m + 1) * P)
+            for i in range(B1):
                 near = [psum.tile([P, BANK], F32, name=f"near{r}", tag="bank") for r in range(NEIGHBOURS)]
                 for r in range(NEIGHBOURS):
                     piece = r * HALVES + c
                     piece_offsets = offsets[:, piece * (BANK // 16) : (piece + 1) * (BANK // 16)]
                     nc.tensor.matmul(
-                        near[r][:], w1n_sb[:, block], x_sb[:].indirect(piece_offsets), start=True, stop=True
+                        near[r][:], w1n_blocks[:, i, :], x_sb[:].indirect(piece_offsets), start=True, stop=True
                     )
                 best = work.tile([P, BANK], F32, name="best")
                 nc.scalar.copy(best[:], near[0][:])
                 for r in range(1, NEIGHBOURS):
                     nc.vector.tensor_max(best[:], near[r][:], best[:])
-                nc.vector.tensor_add(best[:], best[:], own[m][:, half])
+                nc.vector.tensor_add(best[:], best[:], own[:, i, half])
                 nc.vector.scalar_tensor_tensor(
-                    out=x1_f32[m][:, half], in0=best[:], scalar=NEG_SLOPE, in1=best[:], op0=ALU.mult, op1=ALU.max
+                    out=x1_f32[:, i, half], in0=best[:], scalar=NEG_SLOPE, in1=best[:], op0=ALU.mult, op1=ALU.max
                 )
-                nc.scalar.copy(x1_bf[m][:, half], x1_f32[m][:, half])
-                nc.sync.dma_start(out[block, half], x1_f32[m][:, half])
+                nc.scalar.copy(x1_bf[:, i, half], x1_f32[:, i, half])
+            nc.sync.dma_start(x1_rows[:, :, half], x1_f32[:, :, half])
 
-        u2_rows = out[F1_BLOCKS * P : (F1_BLOCKS + F2_BLOCKS) * P, :].rearrange("(q p) n -> p q n", p=P)
-        t2_rows = out[(F1_BLOCKS + F2_BLOCKS) * P :, :].rearrange("(q p) n -> p q n", p=P)
-        for c in range(HALVES):
-            half = slice(c * BANK, (c + 1) * BANK)
-            for g in range(F2_BLOCKS // GROUP):
-                u2_sb = stage.tile([P, GROUP, BANK], F32, name="u2_sb")
-                t2_sb = stage.tile([P, GROUP, BANK], F32, name="t2_sb")
-                for i in range(GROUP):
-                    q = g * GROUP + i
-                    block = slice(q * P, (q + 1) * P)
+        w2n_blocks = w2n_sb[:].rearrange("p k (j i) -> p k i j", i=B2)
+        w2c_blocks = w2c_sb[:].rearrange("p k (j i) -> p k i j", i=B2)
+        u2_rows = out[B1 * P : (B1 + B2) * P, :].rearrange("(p i) n -> p i n", i=B2)
+        t2_rows = out[(B1 + B2) * P :, :].rearrange("(p i) n -> p i n", i=B2)
+        for g in range(B2 // GROUP):
+            u2_sb = stage.tile([P, GROUP, NODES], F32, name="u2_sb")
+            t2_sb = stage.tile([P, GROUP, NODES], F32, name="t2_sb")
+            for c in range(HALVES):
+                half = slice(c * BANK, (c + 1) * BANK)
+                for j in range(GROUP):
+                    i = g * GROUP + j
                     u2_bank = psum.tile([P, BANK], F32, name="u2_bank", tag="bank")
                     c2_bank = psum.tile([P, BANK], F32, name="c2_bank", tag="bank")
-                    for k in range(F1_BLOCKS):
-                        first, last = k == 0, k == F1_BLOCKS - 1
-                        nc.tensor.matmul(u2_bank[:], w2n_sb[:, k, block], x1_bf[k][:, half], start=first, stop=last)
-                    for k in range(F1_BLOCKS):
-                        first, last = k == 0, k == F1_BLOCKS - 1
-                        nc.tensor.matmul(c2_bank[:], w2c_sb[:, k, block], x1_bf[k][:, half], start=first, stop=last)
-                    nc.scalar.copy(u2_sb[:, i, :], u2_bank[:])
+                    for k in range(B1):
+                        nc.tensor.matmul(
+                            u2_bank[:], w2n_blocks[:, k, i, :], x1_bf[:, k, half], start=(k == 0), stop=(k == B1 - 1)
+                        )
+                    for k in range(B1):
+                        nc.tensor.matmul(
+                            c2_bank[:], w2c_blocks[:, k, i, :], x1_bf[:, k, half], start=(k == 0), stop=(k == B1 - 1)
+                        )
+                    nc.scalar.copy(u2_sb[:, j, half], u2_bank[:])
                     nc.vector.scalar_tensor_tensor(
-                        out=t2_sb[:, i, :],
+                        out=t2_sb[:, j, half],
                         in0=c2_bank[:],
-                        scalar=bias_cols[:, q : q + 1],
-                        in1=u2_sb[:, i, :],
+                        scalar=b2_cols[:, i : i + 1],
+                        in1=u2_sb[:, j, half],
                         op0=ALU.add,
                         op1=ALU.subtract,
                     )
-                group = slice(g * GROUP, (g + 1) * GROUP)
-                nc.sync.dma_start(u2_rows[:, group, half], u2_sb[:])
-                nc.sync.dma_start(t2_rows[:, group, half], t2_sb[:])
+            group = slice(g * GROUP, (g + 1) * GROUP)
+            nc.sync.dma_start(u2_rows[:, group, :], u2_sb[:])
+            nc.sync.dma_start(t2_rows[:, group, :], t2_sb[:])

@@ -12,6 +12,7 @@ HALVES = NODES // BANK
 B1 = 2
 B2 = 16
 GROUP = 2
+EARLY = 4
 NEG_SLOPE = 0.2
 
 FLOPS = 2 * P * 256 * (NEIGHBOURS * NODES) + 2 * 2 * P * 256 * NODES + 2 * 2 * 256 * 2048 * NODES
@@ -22,6 +23,7 @@ def tile_skeletonconv_b_kernel(tc, x, w1n, w1c, b1, w2n, w2c, b2, offs, out):
     with (
         tc.tile_pool(name="held", bufs=1) as held,
         tc.tile_pool(name="work", bufs=3) as work,
+        tc.tile_pool(name="halves", bufs=6) as halves,
         tc.tile_pool(name="stage", bufs=4) as stage,
         tc.psum_pool(name="psum", bufs=8) as psum,
     ):
@@ -75,9 +77,10 @@ def tile_skeletonconv_b_kernel(tc, x, w1n, w1c, b1, w2n, w2c, b2, offs, out):
                 nc.scalar.copy(best[:], near[0][:])
                 for r in range(1, NEIGHBOURS):
                     nc.vector.tensor_max(best[:], near[r][:], best[:])
-                nc.vector.tensor_add(best[:], best[:], own[:, i, half])
+                h_max = best
+                nc.vector.tensor_add(h_max[:], best[:], own[:, i, half])
                 nc.vector.scalar_tensor_tensor(
-                    out=x1_f32[:, i, half], in0=best[:], scalar=NEG_SLOPE, in1=best[:], op0=ALU.mult, op1=ALU.max
+                    out=x1_f32[:, i, half], in0=h_max[:], scalar=NEG_SLOPE, in1=h_max[:], op0=ALU.mult, op1=ALU.max
                 )
                 nc.scalar.copy(x1_bf[:, i, half], x1_f32[:, i, half])
             nc.sync.dma_start(x1_rows[:, :, half], x1_f32[:, :, half])
@@ -86,32 +89,43 @@ def tile_skeletonconv_b_kernel(tc, x, w1n, w1c, b1, w2n, w2c, b2, offs, out):
         w2c_blocks = w2c_sb[:].rearrange("p k (j i) -> p k i j", i=B2)
         u2_rows = out[B1 * P : (B1 + B2) * P, :].rearrange("(p i) n -> p i n", i=B2)
         t2_rows = out[(B1 + B2) * P :, :].rearrange("(p i) n -> p i n", i=B2)
-        for g in range(B2 // GROUP):
+
+        def project(i, half, u2_dst, t2_dst):
+            u2_bank = psum.tile([P, BANK], F32, name="u2_bank", tag="bank")
+            c2_bank = psum.tile([P, BANK], F32, name="c2_bank", tag="bank")
+            for k in range(B1):
+                nc.tensor.matmul(
+                    u2_bank[:], w2n_blocks[:, k, i, :], x1_bf[:, k, half], start=(k == 0), stop=(k == B1 - 1)
+                )
+            for k in range(B1):
+                nc.tensor.matmul(
+                    c2_bank[:], w2c_blocks[:, k, i, :], x1_bf[:, k, half], start=(k == 0), stop=(k == B1 - 1)
+                )
+            nc.scalar.copy(u2_dst, u2_bank[:])
+            nc.vector.scalar_tensor_tensor(
+                out=t2_dst, in0=c2_bank[:], scalar=b2_cols[:, i : i + 1], in1=u2_dst, op0=ALU.add, op1=ALU.subtract
+            )
+
+        def half_rows(c):
+            half = slice(c * BANK, (c + 1) * BANK)
+            for i in range(EARLY):
+                u2_half = halves.tile([P, BANK], F32, name="u2_half")
+                t2_half = halves.tile([P, BANK], F32, name="t2_half")
+                project(i, half, u2_half[:], t2_half[:])
+                nc.sync.dma_start(u2_rows[:, i, half], u2_half[:])
+                nc.sync.dma_start(t2_rows[:, i, half], t2_half[:])
+
+        half_rows(0)
+
+        for g in range(EARLY // GROUP, B2 // GROUP):
             u2_sb = stage.tile([P, GROUP, NODES], F32, name="u2_sb")
             t2_sb = stage.tile([P, GROUP, NODES], F32, name="t2_sb")
-            for c in range(HALVES):
-                half = slice(c * BANK, (c + 1) * BANK)
-                for j in range(GROUP):
-                    i = g * GROUP + j
-                    u2_bank = psum.tile([P, BANK], F32, name="u2_bank", tag="bank")
-                    c2_bank = psum.tile([P, BANK], F32, name="c2_bank", tag="bank")
-                    for k in range(B1):
-                        nc.tensor.matmul(
-                            u2_bank[:], w2n_blocks[:, k, i, :], x1_bf[:, k, half], start=(k == 0), stop=(k == B1 - 1)
-                        )
-                    for k in range(B1):
-                        nc.tensor.matmul(
-                            c2_bank[:], w2c_blocks[:, k, i, :], x1_bf[:, k, half], start=(k == 0), stop=(k == B1 - 1)
-                        )
-                    nc.scalar.copy(u2_sb[:, j, half], u2_bank[:])
-                    nc.vector.scalar_tensor_tensor(
-                        out=t2_sb[:, j, half],
-                        in0=c2_bank[:],
-                        scalar=b2_cols[:, i : i + 1],
-                        in1=u2_sb[:, j, half],
-                        op0=ALU.add,
-                        op1=ALU.subtract,
-                    )
+            for j in range(GROUP):
+                for c in range(HALVES):
+                    half = slice(c * BANK, (c + 1) * BANK)
+                    project(g * GROUP + j, half, u2_sb[:, j, half], t2_sb[:, j, half])
             group = slice(g * GROUP, (g + 1) * GROUP)
             nc.sync.dma_start(u2_rows[:, group, :], u2_sb[:])
             nc.sync.dma_start(t2_rows[:, group, :], t2_sb[:])
+
+        half_rows(1)

@@ -14,6 +14,7 @@ B2 = 16
 GROUP = 2
 EARLY = 4
 NEG_SLOPE = 0.2
+WARM_UP = 5
 
 FLOPS = 2 * P * 256 * (NEIGHBOURS * NODES) + 2 * 2 * P * 256 * NODES + 2 * 2 * 256 * 2048 * NODES
 
@@ -43,6 +44,12 @@ def tile_skeletonconv_b_kernel(tc, x, w1n, w1c, b1, w2n, w2c, b2, offs, out):
         nc.sync.dma_start(w2n_sb[:], w2n.rearrange("(p k) q -> p k q", k=B1))
         w2c_sb = held.tile([P, B1, B2 * P], BF16, name="w2c_sb")
         nc.scalar.dma_start(w2c_sb[:], w2c.rearrange("(p k) q -> p k q", k=B1))
+
+        zeros = held.tile([P, BANK], BF16, name="zeros")
+        nc.vector.memset(zeros[:], 0.0)
+        warm_bank = psum.tile([P, BANK], F32, name="warm_bank", tag="bank")
+        for w in range(WARM_UP):
+            nc.tensor.matmul(warm_bank[:], zeros[:, 0:P], zeros[:], start=True, stop=True)
 
         w1n_blocks = held.tile([P, B1, P], BF16, name="w1n_blocks")
         nc.vector.tensor_copy(w1n_blocks[:], w1n_sb[:].rearrange("p (j i) -> p i j", i=B1))

@@ -97,42 +97,46 @@ def tile_skeletonconv_b_kernel(tc, x, w1n, w1c, b1, w2n, w2c, b2, offs, out):
         u2_rows = out[B1 * P : (B1 + B2) * P, :].rearrange("(p i) n -> p i n", i=B2)
         t2_rows = out[(B1 + B2) * P :, :].rearrange("(p i) n -> p i n", i=B2)
 
-        def project(i, half, u2_dst, t2_dst):
+        def project_u2(i, half, u2_dst):
             u2_bank = psum.tile([P, BANK], F32, name="u2_bank", tag="bank")
-            c2_bank = psum.tile([P, BANK], F32, name="c2_bank", tag="bank")
             for k in range(B1):
                 nc.tensor.matmul(
                     u2_bank[:], w2n_blocks[:, k, i, :], x1_bf[:, k, half], start=(k == 0), stop=(k == B1 - 1)
                 )
+            nc.scalar.copy(u2_dst, u2_bank[:])
+
+        def project_t2(i, half, u2_src, t2_dst):
+            c2_bank = psum.tile([P, BANK], F32, name="c2_bank", tag="bank")
             for k in range(B1):
                 nc.tensor.matmul(
                     c2_bank[:], w2c_blocks[:, k, i, :], x1_bf[:, k, half], start=(k == 0), stop=(k == B1 - 1)
                 )
-            nc.scalar.copy(u2_dst, u2_bank[:])
             nc.vector.scalar_tensor_tensor(
-                out=t2_dst, in0=c2_bank[:], scalar=b2_cols[:, i : i + 1], in1=u2_dst, op0=ALU.add, op1=ALU.subtract
+                out=t2_dst, in0=c2_bank[:], scalar=b2_cols[:, i : i + 1], in1=u2_src, op0=ALU.add, op1=ALU.subtract
             )
 
         def half_rows(c):
             half = slice(c * BANK, (c + 1) * BANK)
             for i in range(EARLY):
                 u2_half = halves.tile([P, BANK], F32, name="u2_half")
-                t2_half = halves.tile([P, BANK], F32, name="t2_half")
-                project(i, half, u2_half[:], t2_half[:])
+                project_u2(i, half, u2_half[:])
                 nc.sync.dma_start(u2_rows[:, i, half], u2_half[:])
+                t2_half = halves.tile([P, BANK], F32, name="t2_half")
+                project_t2(i, half, u2_half[:], t2_half[:])
                 nc.sync.dma_start(t2_rows[:, i, half], t2_half[:])
 
         half_rows(0)
 
         for g in range(EARLY // GROUP, B2 // GROUP):
-            u2_sb = stage.tile([P, GROUP, NODES], F32, name="u2_sb")
-            t2_sb = stage.tile([P, GROUP, NODES], F32, name="t2_sb")
-            for j in range(GROUP):
-                for c in range(HALVES):
-                    half = slice(c * BANK, (c + 1) * BANK)
-                    project(g * GROUP + j, half, u2_sb[:, j, half], t2_sb[:, j, half])
             group = slice(g * GROUP, (g + 1) * GROUP)
-            nc.sync.dma_start(u2_rows[:, group, :], u2_sb[:])
+            pieces = [(j, slice(c * BANK, (c + 1) * BANK)) for j in range(GROUP) for c in range(HALVES)]
+            u2_sb = stage.tile([P, GROUP, NODES], F32, name="u2_sb")
+            for j, half in pieces:
+                project_u2(g * GROUP + j, half, u2_sb[:, j, half])
+            nc.scalar.dma_start(u2_rows[:, group, :], u2_sb[:])
+            t2_sb = stage.tile([P, GROUP, NODES], F32, name="t2_sb")
+            for j, half in pieces:
+                project_t2(g * GROUP + j, half, u2_sb[:, j, half], t2_sb[:, j, half])
             nc.sync.dma_start(t2_rows[:, group, :], t2_sb[:])
 
         half_rows(1)

@@ -70,9 +70,12 @@ def tile_skeletonconv_b_kernel(tc, x, w1n, w1c, b1, w2n, w2c, b2, offs, out):
         x1_rows = out[0 : B1 * P, :].rearrange("(p i) n -> p i n", i=B1)
         x1_f32 = held.tile([P, B1, NODES], F32, name="x1_f32")
         x1_bf = held.tile([P, B1, NODES], BF16, name="x1_bf")
-        for c in range(HALVES):
-            half = slice(c * BANK, (c + 1) * BANK)
-            for i in range(B1):
+        groups = [(c, i) for c in range(HALVES) for i in range(B1)]
+        for g in range(len(groups) + 1):
+            begin = g < len(groups)
+            finish = g > 0
+            if begin:
+                c, i = groups[g]
                 near = [psum.tile([P, BANK], F32, name=f"near{r}", tag="bank") for r in range(NEIGHBOURS)]
                 for r in range(NEIGHBOURS):
                     piece = r * HALVES + c
@@ -80,17 +83,27 @@ def tile_skeletonconv_b_kernel(tc, x, w1n, w1c, b1, w2n, w2c, b2, offs, out):
                     nc.tensor.matmul(
                         near[r][:], w1n_blocks[:, i, :], x_sb[:].indirect(piece_offsets), start=True, stop=True
                     )
-                best = work.tile([P, BANK], F32, name="best")
-                nc.scalar.copy(best[:], near[0][:])
-                for r in range(1, NEIGHBOURS):
-                    nc.vector.tensor_max(best[:], near[r][:], best[:])
-                h_max = best
-                nc.vector.tensor_add(h_max[:], best[:], own[:, i, half])
+                best01 = work.tile([P, BANK], F32, name="best01")
+                nc.scalar.copy(best01[:], near[0][:])
+                best23 = work.tile([P, BANK], F32, name="best23")
+                nc.scalar.copy(best23[:], near[2][:])
+            if finish:
+                nc.vector.tensor_max(h_max[:], h_max[:], h_other[:])
+            if begin:
+                nc.vector.tensor_max(best01[:], near[1][:], best01[:])
+            if finish:
+                nc.vector.tensor_add(h_max[:], h_max[:], own[:, h_i, h_half])
+            if begin:
+                nc.vector.tensor_max(best23[:], near[3][:], best23[:])
+            if finish:
                 nc.vector.scalar_tensor_tensor(
-                    out=x1_f32[:, i, half], in0=h_max[:], scalar=NEG_SLOPE, in1=h_max[:], op0=ALU.mult, op1=ALU.max
+                    out=x1_f32[:, h_i, h_half], in0=h_max[:], scalar=NEG_SLOPE, in1=h_max[:], op0=ALU.mult, op1=ALU.max
                 )
-                nc.scalar.copy(x1_bf[:, i, half], x1_f32[:, i, half])
-            nc.sync.dma_start(x1_rows[:, :, half], x1_f32[:, :, half])
+                nc.scalar.copy(x1_bf[:, h_i, h_half], x1_f32[:, h_i, h_half])
+                if h_i == B1 - 1:
+                    nc.sync.dma_start(x1_rows[:, :, h_half], x1_f32[:, :, h_half])
+            if begin:
+                h_max, h_other, h_i, h_half = best01, best23, i, slice(c * BANK, (c + 1) * BANK)
 
         w2n_blocks = w2n_sb[:].rearrange("p k (j i) -> p k i j", i=B2)
         w2c_blocks = w2c_sb[:].rearrange("p k (j i) -> p k i j", i=B2)

@@ -2,7 +2,6 @@ import concourse.mybir as mybir
 
 BF16, F32, U16 = mybir.dt.bfloat16, mybir.dt.float32, mybir.dt.uint16
 ALU = mybir.AluOpType
-ACT = mybir.ActivationFunctionType
 
 P = 128
 NODES = 1024
@@ -12,7 +11,7 @@ HALVES = NODES // BANK
 B1 = 2
 B2 = 16
 GROUP = 2
-EARLY = 4
+EARLY = 6
 NEG_SLOPE = 0.2
 WARM_UP = 5
 
@@ -24,7 +23,7 @@ def tile_skeletonconv_b_kernel(tc, x, w1n, w1c, b1, w2n, w2c, b2, offs, out):
     with (
         tc.tile_pool(name="held", bufs=1) as held,
         tc.tile_pool(name="work", bufs=3) as work,
-        tc.tile_pool(name="halves", bufs=6) as halves,
+        tc.tile_pool(name="halves", bufs=8) as halves,
         tc.tile_pool(name="stage", bufs=4) as stage,
         tc.psum_pool(name="psum", bufs=8) as psum,
     ):
@@ -58,14 +57,15 @@ def tile_skeletonconv_b_kernel(tc, x, w1n, w1c, b1, w2n, w2c, b2, offs, out):
         w1c_blocks = held.tile([P, B1, P], BF16, name="w1c_blocks")
         nc.vector.tensor_copy(w1c_blocks[:], w1c_sb[:].rearrange("p (j i) -> p i j", i=B1))
 
-        own = held.tile([P, B1, NODES], F32, name="own")
-        for c in range(HALVES):
+        def centre_term(c):
             half = slice(c * BANK, (c + 1) * BANK)
+            banks = [psum.tile([P, BANK], F32, name=f"own_bank{i}", tag="bank") for i in range(B1)]
             for i in range(B1):
-                own_bank = psum.tile([P, BANK], F32, name="own_bank", tag="bank")
-                nc.tensor.matmul(own_bank[:], w1c_blocks[:, i, :], x_sb[:, half], start=True, stop=False)
-                nc.tensor.matmul(own_bank[:], w1n_neg_blocks[:, i, :], x_sb[:, half], start=False, stop=True)
-                nc.scalar.activation(own[:, i, half], own_bank[:], ACT.Identity, bias=b1_cols[:, i : i + 1])
+                nc.tensor.matmul(banks[i][:], w1c_blocks[:, i, :], x_sb[:, half], start=True, stop=False)
+                nc.tensor.matmul(banks[i][:], w1n_neg_blocks[:, i, :], x_sb[:, half], start=False, stop=True)
+            return banks
+
+        own_banks = [centre_term(0)]
 
         x1_rows = out[0 : B1 * P, :].rearrange("(p i) n -> p i n", i=B1)
         x1_f32 = held.tile([P, B1, NODES], F32, name="x1_f32")
@@ -87,12 +87,17 @@ def tile_skeletonconv_b_kernel(tc, x, w1n, w1c, b1, w2n, w2c, b2, offs, out):
                 nc.scalar.copy(best01[:], near[0][:])
                 best23 = work.tile([P, BANK], F32, name="best23")
                 nc.scalar.copy(best23[:], near[2][:])
+                if g == len(groups) - 1:
+                    own_banks.append(centre_term(1))
             if finish:
+                h_own = own_banks[h_c][h_i]
                 nc.vector.tensor_max(h_max[:], h_max[:], h_other[:])
             if begin:
                 nc.vector.tensor_max(best01[:], near[1][:], best01[:])
             if finish:
-                nc.vector.tensor_add(h_max[:], h_max[:], own[:, h_i, h_half])
+                nc.vector.scalar_tensor_tensor(
+                    out=h_max[:], in0=h_own[:], scalar=b1_cols[:, h_i : h_i + 1], in1=h_max[:], op0=ALU.add, op1=ALU.add
+                )
             if begin:
                 nc.vector.tensor_max(best23[:], near[3][:], best23[:])
             if finish:
@@ -103,7 +108,7 @@ def tile_skeletonconv_b_kernel(tc, x, w1n, w1c, b1, w2n, w2c, b2, offs, out):
                 if h_i == B1 - 1:
                     nc.sync.dma_start(x1_rows[:, :, h_half], x1_f32[:, :, h_half])
             if begin:
-                h_max, h_other, h_i, h_half = best01, best23, i, slice(c * BANK, (c + 1) * BANK)
+                h_max, h_other, h_c, h_i, h_half = best01, best23, c, i, slice(c * BANK, (c + 1) * BANK)
 
         w2n_blocks = w2n_sb[:].rearrange("p k (j i) -> p k i j", i=B2)
         w2c_blocks = w2c_sb[:].rearrange("p k (j i) -> p k i j", i=B2)
@@ -130,12 +135,13 @@ def tile_skeletonconv_b_kernel(tc, x, w1n, w1c, b1, w2n, w2c, b2, offs, out):
 
         def half_rows(c):
             half = slice(c * BANK, (c + 1) * BANK)
+            u2_halves = [halves.tile([P, BANK], F32, name="u2_half") for i in range(EARLY)]
             for i in range(EARLY):
-                u2_half = halves.tile([P, BANK], F32, name="u2_half")
-                project_u2(i, half, u2_half[:])
-                nc.sync.dma_start(u2_rows[:, i, half], u2_half[:])
+                project_u2(i, half, u2_halves[i][:])
+                nc.sync.dma_start(u2_rows[:, i, half], u2_halves[i][:])
+            for i in range(EARLY):
                 t2_half = halves.tile([P, BANK], F32, name="t2_half")
-                project_t2(i, half, u2_half[:], t2_half[:])
+                project_t2(i, half, u2_halves[i][:], t2_half[:])
                 nc.sync.dma_start(t2_rows[:, i, half], t2_half[:])
 
         half_rows(0)

@@ -13,7 +13,7 @@ B2 = 16
 GROUP = 2
 EARLY = 6
 NEG_SLOPE = 0.2
-WARM_UP = 5
+WARM_UP = 4
 
 FLOPS = 2 * P * 256 * (NEIGHBOURS * NODES) + 2 * 2 * P * 256 * NODES + 2 * 2 * 256 * 2048 * NODES
 
@@ -36,13 +36,13 @@ def tile_skeletonconv_b_kernel(tc, x, w1n, w1c, b1, w2n, w2c, b2, offs, out):
         w1c_sb = held.tile([P, B1 * P], BF16, name="w1c_sb")
         nc.sync.dma_start(w1c_sb[:], w1c)
         b1_cols = held.tile([P, B1], F32, name="b1_cols")
-        nc.scalar.dma_start(b1_cols[:], b1.rearrange("(p i) o -> p (i o)", i=B1))
+        nc.scalar.dma_start(b1_cols[:], b1.rearrange("(i p) o -> p (i o)", p=P))
         b2_cols = held.tile([P, B2], F32, name="b2_cols")
         nc.scalar.dma_start(b2_cols[:], b2.rearrange("(p i) o -> p (i o)", i=B2))
         w2n_sb = held.tile([P, B1, B2 * P], BF16, name="w2n_sb")
-        nc.sync.dma_start(w2n_sb[:], w2n.rearrange("(p k) q -> p k q", k=B1))
+        nc.sync.dma_start(w2n_sb[:], w2n.rearrange("(k p) q -> p k q", p=P))
         w2c_sb = held.tile([P, B1, B2 * P], BF16, name="w2c_sb")
-        nc.scalar.dma_start(w2c_sb[:], w2c.rearrange("(p k) q -> p k q", k=B1))
+        nc.scalar.dma_start(w2c_sb[:], w2c.rearrange("(k p) q -> p k q", p=P))
 
         zeros = held.tile([P, BANK], BF16, name="zeros")
         nc.vector.memset(zeros[:], 0.0)
@@ -50,12 +50,11 @@ def tile_skeletonconv_b_kernel(tc, x, w1n, w1c, b1, w2n, w2c, b2, offs, out):
         for w in range(WARM_UP):
             nc.tensor.matmul(warm_bank[:], zeros[:, 0:P], zeros[:], start=True, stop=True)
 
-        w1n_blocks = held.tile([P, B1, P], BF16, name="w1n_blocks")
-        nc.vector.tensor_copy(w1n_blocks[:], w1n_sb[:].rearrange("p (j i) -> p i j", i=B1))
-        w1n_neg_blocks = held.tile([P, B1, P], BF16, name="w1n_neg_blocks")
-        nc.vector.tensor_scalar_mul(w1n_neg_blocks[:], w1n_sb[:].rearrange("p (j i) -> p i j", i=B1), -1.0)
-        w1c_blocks = held.tile([P, B1, P], BF16, name="w1c_blocks")
-        nc.vector.tensor_copy(w1c_blocks[:], w1c_sb[:].rearrange("p (j i) -> p i j", i=B1))
+        w1n_neg = held.tile([P, B1 * P], BF16, name="w1n_neg")
+        nc.vector.tensor_scalar_mul(w1n_neg[:], w1n_sb[:], -1.0)
+        w1n_blocks = w1n_sb[:].rearrange("p (i j) -> p i j", i=B1)
+        w1n_neg_blocks = w1n_neg[:].rearrange("p (i j) -> p i j", i=B1)
+        w1c_blocks = w1c_sb[:].rearrange("p (i j) -> p i j", i=B1)
 
         def centre_term(c):
             half = slice(c * BANK, (c + 1) * BANK)
@@ -67,7 +66,7 @@ def tile_skeletonconv_b_kernel(tc, x, w1n, w1c, b1, w2n, w2c, b2, offs, out):
 
         own_banks = [centre_term(0)]
 
-        x1_rows = out[0 : B1 * P, :].rearrange("(p i) n -> p i n", i=B1)
+        x1_rows = out[0 : B1 * P, :].rearrange("(i p) n -> p i n", p=P)
         x1_f32 = held.tile([P, B1, NODES], F32, name="x1_f32")
         x1_bf = held.tile([P, B1, NODES], BF16, name="x1_bf")
         groups = [(c, i) for c in range(HALVES) for i in range(B1)]
@@ -115,47 +114,53 @@ def tile_skeletonconv_b_kernel(tc, x, w1n, w1c, b1, w2n, w2c, b2, offs, out):
         u2_rows = out[B1 * P : (B1 + B2) * P, :].rearrange("(p i) n -> p i n", i=B2)
         t2_rows = out[(B1 + B2) * P :, :].rearrange("(p i) n -> p i n", i=B2)
 
-        def project_u2(i, half, u2_dst):
-            u2_bank = psum.tile([P, BANK], F32, name="u2_bank", tag="bank")
+        def project(weight_blocks, i, node_halves):
+            banks = [psum.tile([P, BANK], F32, name=f"bank{n}", tag="bank") for n in range(len(node_halves))]
             for k in range(B1):
-                nc.tensor.matmul(
-                    u2_bank[:], w2n_blocks[:, k, i, :], x1_bf[:, k, half], start=(k == 0), stop=(k == B1 - 1)
-                )
-            nc.scalar.copy(u2_dst, u2_bank[:])
+                for bank, half in zip(banks, node_halves):
+                    nc.tensor.matmul(
+                        bank[:], weight_blocks[:, k, i, :], x1_bf[:, k, half], start=(k == 0), stop=(k == B1 - 1)
+                    )
+            return banks
 
-        def project_t2(i, half, u2_src, t2_dst):
-            c2_bank = psum.tile([P, BANK], F32, name="c2_bank", tag="bank")
-            for k in range(B1):
-                nc.tensor.matmul(
-                    c2_bank[:], w2c_blocks[:, k, i, :], x1_bf[:, k, half], start=(k == 0), stop=(k == B1 - 1)
+        def project_u2(i, node_halves, u2_dsts):
+            for u2_bank, u2_dst in zip(project(w2n_blocks, i, node_halves), u2_dsts):
+                nc.scalar.copy(u2_dst, u2_bank[:])
+
+        def project_t2(i, node_halves, u2_srcs, t2_dsts):
+            for c2_bank, u2_src, t2_dst in zip(project(w2c_blocks, i, node_halves), u2_srcs, t2_dsts):
+                nc.vector.scalar_tensor_tensor(
+                    out=t2_dst, in0=c2_bank[:], scalar=b2_cols[:, i : i + 1], in1=u2_src, op0=ALU.add, op1=ALU.subtract
                 )
-            nc.vector.scalar_tensor_tensor(
-                out=t2_dst, in0=c2_bank[:], scalar=b2_cols[:, i : i + 1], in1=u2_src, op0=ALU.add, op1=ALU.subtract
-            )
 
         def half_rows(c):
             half = slice(c * BANK, (c + 1) * BANK)
             u2_halves = [halves.tile([P, BANK], F32, name="u2_half") for i in range(EARLY)]
             for i in range(EARLY):
-                project_u2(i, half, u2_halves[i][:])
+                project_u2(i, [half], [u2_halves[i][:]])
                 nc.sync.dma_start(u2_rows[:, i, half], u2_halves[i][:])
             for i in range(EARLY):
                 t2_half = halves.tile([P, BANK], F32, name="t2_half")
-                project_t2(i, half, u2_halves[i][:], t2_half[:])
+                project_t2(i, [half], [u2_halves[i][:]], [t2_half[:]])
                 nc.sync.dma_start(t2_rows[:, i, half], t2_half[:])
 
         half_rows(0)
 
+        both_halves = [slice(c * BANK, (c + 1) * BANK) for c in range(HALVES)]
         for g in range(EARLY // GROUP, B2 // GROUP):
             group = slice(g * GROUP, (g + 1) * GROUP)
-            pieces = [(j, slice(c * BANK, (c + 1) * BANK)) for j in range(GROUP) for c in range(HALVES)]
             u2_sb = stage.tile([P, GROUP, NODES], F32, name="u2_sb")
-            for j, half in pieces:
-                project_u2(g * GROUP + j, half, u2_sb[:, j, half])
+            for j in range(GROUP):
+                project_u2(g * GROUP + j, both_halves, [u2_sb[:, j, half] for half in both_halves])
             nc.scalar.dma_start(u2_rows[:, group, :], u2_sb[:])
             t2_sb = stage.tile([P, GROUP, NODES], F32, name="t2_sb")
-            for j, half in pieces:
-                project_t2(g * GROUP + j, half, u2_sb[:, j, half], t2_sb[:, j, half])
+            for j in range(GROUP):
+                project_t2(
+                    g * GROUP + j,
+                    both_halves,
+                    [u2_sb[:, j, half] for half in both_halves],
+                    [t2_sb[:, j, half] for half in both_halves],
+                )
             nc.sync.dma_start(t2_rows[:, group, :], t2_sb[:])
 
         half_rows(1)

@@ -11,7 +11,7 @@ HALVES = NODES // BANK
 B1 = 2
 B2 = 16
 GROUP = 2
-EARLY = 6
+EARLY = 4
 NEG_SLOPE = 0.2
 WARM_UP = 4
 

@@ -114,53 +114,47 @@ def tile_skeletonconv_b_kernel(tc, x, w1n, w1c, b1, w2n, w2c, b2, offs, out):
         u2_rows = out[B1 * P : (B1 + B2) * P, :].rearrange("(p i) n -> p i n", i=B2)
         t2_rows = out[(B1 + B2) * P :, :].rearrange("(p i) n -> p i n", i=B2)
 
-        def project(weight_blocks, i, node_halves):
-            banks = [psum.tile([P, BANK], F32, name=f"bank{n}", tag="bank") for n in range(len(node_halves))]
+        def project_u2(i, half, u2_dst):
+            u2_bank = psum.tile([P, BANK], F32, name="u2_bank", tag="bank")
             for k in range(B1):
-                for bank, half in zip(banks, node_halves):
-                    nc.tensor.matmul(
-                        bank[:], weight_blocks[:, k, i, :], x1_bf[:, k, half], start=(k == 0), stop=(k == B1 - 1)
-                    )
-            return banks
-
-        def project_u2(i, node_halves, u2_dsts):
-            for u2_bank, u2_dst in zip(project(w2n_blocks, i, node_halves), u2_dsts):
-                nc.scalar.copy(u2_dst, u2_bank[:])
-
-        def project_t2(i, node_halves, u2_srcs, t2_dsts):
-            for c2_bank, u2_src, t2_dst in zip(project(w2c_blocks, i, node_halves), u2_srcs, t2_dsts):
-                nc.vector.scalar_tensor_tensor(
-                    out=t2_dst, in0=c2_bank[:], scalar=b2_cols[:, i : i + 1], in1=u2_src, op0=ALU.add, op1=ALU.subtract
+                nc.tensor.matmul(
+                    u2_bank[:], w2n_blocks[:, k, i, :], x1_bf[:, k, half], start=(k == 0), stop=(k == B1 - 1)
                 )
+            nc.scalar.copy(u2_dst, u2_bank[:])
+
+        def project_t2(i, half, u2_src, t2_dst):
+            c2_bank = psum.tile([P, BANK], F32, name="c2_bank", tag="bank")
+            for k in range(B1):
+                nc.tensor.matmul(
+                    c2_bank[:], w2c_blocks[:, k, i, :], x1_bf[:, k, half], start=(k == 0), stop=(k == B1 - 1)
+                )
+            nc.vector.scalar_tensor_tensor(
+                out=t2_dst, in0=c2_bank[:], scalar=b2_cols[:, i : i + 1], in1=u2_src, op0=ALU.add, op1=ALU.subtract
+            )
 
         def half_rows(c):
             half = slice(c * BANK, (c + 1) * BANK)
             u2_halves = [halves.tile([P, BANK], F32, name="u2_half") for i in range(EARLY)]
             for i in range(EARLY):
-                project_u2(i, [half], [u2_halves[i][:]])
+                project_u2(i, half, u2_halves[i][:])
                 nc.sync.dma_start(u2_rows[:, i, half], u2_halves[i][:])
             for i in range(EARLY):
                 t2_half = halves.tile([P, BANK], F32, name="t2_half")
-                project_t2(i, [half], [u2_halves[i][:]], [t2_half[:]])
+                project_t2(i, half, u2_halves[i][:], t2_half[:])
                 nc.sync.dma_start(t2_rows[:, i, half], t2_half[:])
 
         half_rows(0)
 
-        both_halves = [slice(c * BANK, (c + 1) * BANK) for c in range(HALVES)]
         for g in range(EARLY // GROUP, B2 // GROUP):
             group = slice(g * GROUP, (g + 1) * GROUP)
+            pieces = [(j, slice(c * BANK, (c + 1) * BANK)) for j in range(GROUP) for c in range(HALVES)]
             u2_sb = stage.tile([P, GROUP, NODES], F32, name="u2_sb")
-            for j in range(GROUP):
-                project_u2(g * GROUP + j, both_halves, [u2_sb[:, j, half] for half in both_halves])
+            for j, half in pieces:
+                project_u2(g * GROUP + j, half, u2_sb[:, j, half])
             nc.scalar.dma_start(u2_rows[:, group, :], u2_sb[:])
             t2_sb = stage.tile([P, GROUP, NODES], F32, name="t2_sb")
-            for j in range(GROUP):
-                project_t2(
-                    g * GROUP + j,
-                    both_halves,
-                    [u2_sb[:, j, half] for half in both_halves],
-                    [t2_sb[:, j, half] for half in both_halves],
-                )
+            for j, half in pieces:
+                project_t2(g * GROUP + j, half, u2_sb[:, j, half], t2_sb[:, j, half])
             nc.sync.dma_start(t2_rows[:, group, :], t2_sb[:])
 
         half_rows(1)

@@ -156,5 +156,5 @@ def tile_skeletonconv_b_kernel(tc, x, w1n, w1c, b1, w2n, w2c, b2, offs, out):
             for j, half in pieces:
                 project_t2(g * GROUP + j, half, u2_sb[:, j, half], t2_sb[:, j, half])
             nc.sync.dma_start(t2_rows[:, group, :], t2_sb[:])
-
-        half_rows(1)
+            if g == EARLY // GROUP:
+                half_rows(1)

@@ -13,7 +13,7 @@ B2 = 16
 GROUP = 2
 EARLY = 4
 NEG_SLOPE = 0.2
-WARM_UP = 4
+WARM_UP = 2
 
 FLOPS = 2 * P * 256 * (NEIGHBOURS * NODES) + 2 * 2 * P * 256 * NODES + 2 * 2 * 256 * 2048 * NODES
 
@@ -27,14 +27,15 @@ def tile_skeletonconv_b_kernel(tc, x, w1n, w1c, b1, w2n, w2c, b2, offs, out):
         tc.tile_pool(name="stage", bufs=4) as stage,
         tc.psum_pool(name="psum", bufs=8) as psum,
     ):
-        offsets = held.tile([P, NEIGHBOURS * NODES // 16], U16, name="offsets")
-        nc.sync.dma_start(offsets[:], offs)
         x_sb = held.tile([P, NODES], BF16, name="x_sb")
-        nc.scalar.dma_start(x_sb[:], x)
-        w1n_sb = held.tile([P, B1 * P], BF16, name="w1n_sb")
-        nc.sync.dma_start(w1n_sb[:], w1n)
         w1c_sb = held.tile([P, B1 * P], BF16, name="w1c_sb")
+        w1n_sb = held.tile([P, B1 * P], BF16, name="w1n_sb")
+        offsets = held.tile([P, NEIGHBOURS * NODES // 16], U16, name="offsets")
+        nc.scalar.dma_start(x_sb[:, 0:BANK], x[:, 0:BANK])
         nc.sync.dma_start(w1c_sb[:], w1c)
+        nc.scalar.dma_start(x_sb[:, BANK:NODES], x[:, BANK:NODES])
+        nc.sync.dma_start(w1n_sb[:], w1n)
+        nc.sync.dma_start(offsets[:], offs)
         b1_cols = held.tile([P, B1], F32, name="b1_cols")
         nc.scalar.dma_start(b1_cols[:], b1.rearrange("(i p) o -> p (i o)", p=P))
         b2_cols = held.tile([P, B2], F32, name="b2_cols")
@@ -61,6 +62,7 @@ def tile_skeletonconv_b_kernel(tc, x, w1n, w1c, b1, w2n, w2c, b2, offs, out):
             banks = [psum.tile([P, BANK], F32, name=f"own_bank{i}", tag="bank") for i in range(B1)]
             for i in range(B1):
                 nc.tensor.matmul(banks[i][:], w1c_blocks[:, i, :], x_sb[:, half], start=True, stop=False)
+            for i in range(B1):
                 nc.tensor.matmul(banks[i][:], w1n_neg_blocks[:, i, :], x_sb[:, half], start=False, stop=True)
             return banks
 

import concourse.mybir as mybir

BF16, F32, U16 = mybir.dt.bfloat16, mybir.dt.float32, mybir.dt.uint16
ALU = mybir.AluOpType

P = 128
NODES = 1024
NEIGHBOURS = 4
BANK = 512
HALVES = NODES // BANK
B1 = 2
B2 = 16
GROUP = 2
EARLY = 4
NEG_SLOPE = 0.2
WARM_UP = 2

FLOPS = 2 * P * 256 * (NEIGHBOURS * NODES) + 2 * 2 * P * 256 * NODES + 2 * 2 * 256 * 2048 * NODES


def tile_skeletonconv_b_kernel(tc, x, w1n, w1c, b1, w2n, w2c, b2, offs, out):
    nc = tc.nc
    with (
        tc.tile_pool(name="held", bufs=1) as held,
        tc.tile_pool(name="work", bufs=3) as work,
        tc.tile_pool(name="halves", bufs=8) as halves,
        tc.tile_pool(name="stage", bufs=4) as stage,
        tc.psum_pool(name="psum", bufs=8) as psum,
    ):
        x_sb = held.tile([P, NODES], BF16, name="x_sb")
        w1c_sb = held.tile([P, B1 * P], BF16, name="w1c_sb")
        w1n_sb = held.tile([P, B1 * P], BF16, name="w1n_sb")
        offsets = held.tile([P, NEIGHBOURS * NODES // 16], U16, name="offsets")
        nc.scalar.dma_start(x_sb[:, 0:BANK], x[:, 0:BANK])
        nc.sync.dma_start(w1c_sb[:], w1c)
        nc.scalar.dma_start(x_sb[:, BANK:NODES], x[:, BANK:NODES])
        nc.sync.dma_start(w1n_sb[:], w1n)
        nc.sync.dma_start(offsets[:], offs)
        b1_cols = held.tile([P, B1], F32, name="b1_cols")
        nc.scalar.dma_start(b1_cols[:], b1.rearrange("(i p) o -> p (i o)", p=P))
        b2_cols = held.tile([P, B2], F32, name="b2_cols")
        nc.scalar.dma_start(b2_cols[:], b2.rearrange("(p i) o -> p (i o)", i=B2))
        w2n_sb = held.tile([P, B1, B2 * P], BF16, name="w2n_sb")
        nc.sync.dma_start(w2n_sb[:], w2n.rearrange("(k p) q -> p k q", p=P))
        w2c_sb = held.tile([P, B1, B2 * P], BF16, name="w2c_sb")
        nc.scalar.dma_start(w2c_sb[:], w2c.rearrange("(k p) q -> p k q", p=P))

        zeros = held.tile([P, BANK], BF16, name="zeros")
        nc.vector.memset(zeros[:], 0.0)
        warm_bank = psum.tile([P, BANK], F32, name="warm_bank", tag="bank")
        for w in range(WARM_UP):
            nc.tensor.matmul(warm_bank[:], zeros[:, 0:P], zeros[:], start=True, stop=True)

        w1n_neg = held.tile([P, B1 * P], BF16, name="w1n_neg")
        nc.vector.tensor_scalar_mul(w1n_neg[:], w1n_sb[:], -1.0)
        w1n_blocks = w1n_sb[:].rearrange("p (i j) -> p i j", i=B1)
        w1n_neg_blocks = w1n_neg[:].rearrange("p (i j) -> p i j", i=B1)
        w1c_blocks = w1c_sb[:].rearrange("p (i j) -> p i j", i=B1)

        def centre_term(c):
            half = slice(c * BANK, (c + 1) * BANK)
            banks = [psum.tile([P, BANK], F32, name=f"own_bank{i}", tag="bank") for i in range(B1)]
            for i in range(B1):
                nc.tensor.matmul(banks[i][:], w1c_blocks[:, i, :], x_sb[:, half], start=True, stop=False)
            for i in range(B1):
                nc.tensor.matmul(banks[i][:], w1n_neg_blocks[:, i, :], x_sb[:, half], start=False, stop=True)
            return banks

        own_banks = [centre_term(0)]

        x1_rows = out[0 : B1 * P, :].rearrange("(i p) n -> p i n", p=P)
        x1_f32 = held.tile([P, B1, NODES], F32, name="x1_f32")
        x1_bf = held.tile([P, B1, NODES], BF16, name="x1_bf")
        groups = [(c, i) for c in range(HALVES) for i in range(B1)]
        for g in range(len(groups) + 1):
            begin = g < len(groups)
            finish = g > 0
            if begin:
                c, i = groups[g]
                near = [psum.tile([P, BANK], F32, name=f"near{r}", tag="bank") for r in range(NEIGHBOURS)]
                for r in range(NEIGHBOURS):
                    piece = r * HALVES + c
                    piece_offsets = offsets[:, piece * (BANK // 16) : (piece + 1) * (BANK // 16)]
                    nc.tensor.matmul(
                        near[r][:], w1n_blocks[:, i, :], x_sb[:].indirect(piece_offsets), start=True, stop=True
                    )
                best01 = work.tile([P, BANK], F32, name="best01")
                nc.scalar.copy(best01[:], near[0][:])
                best23 = work.tile([P, BANK], F32, name="best23")
                nc.scalar.copy(best23[:], near[2][:])
                if g == len(groups) - 1:
                    own_banks.append(centre_term(1))
            if finish:
                h_own = own_banks[h_c][h_i]
                nc.vector.tensor_max(h_max[:], h_max[:], h_other[:])
            if begin:
                nc.vector.tensor_max(best01[:], near[1][:], best01[:])
            if finish:
                nc.vector.scalar_tensor_tensor(
                    out=h_max[:], in0=h_own[:], scalar=b1_cols[:, h_i : h_i + 1], in1=h_max[:], op0=ALU.add, op1=ALU.add
                )
            if begin:
                nc.vector.tensor_max(best23[:], near[3][:], best23[:])
            if finish:
                nc.vector.scalar_tensor_tensor(
                    out=x1_f32[:, h_i, h_half], in0=h_max[:], scalar=NEG_SLOPE, in1=h_max[:], op0=ALU.mult, op1=ALU.max
                )
                nc.scalar.copy(x1_bf[:, h_i, h_half], x1_f32[:, h_i, h_half])
                if h_i == B1 - 1:
                    nc.sync.dma_start(x1_rows[:, :, h_half], x1_f32[:, :, h_half])
            if begin:
                h_max, h_other, h_c, h_i, h_half = best01, best23, c, i, slice(c * BANK, (c + 1) * BANK)

        w2n_blocks = w2n_sb[:].rearrange("p k (j i) -> p k i j", i=B2)
        w2c_blocks = w2c_sb[:].rearrange("p k (j i) -> p k i j", i=B2)
        u2_rows = out[B1 * P : (B1 + B2) * P, :].rearrange("(p i) n -> p i n", i=B2)
        t2_rows = out[(B1 + B2) * P :, :].rearrange("(p i) n -> p i n", i=B2)

        def project_u2(i, half, u2_dst):
            u2_bank = psum.tile([P, BANK], F32, name="u2_bank", tag="bank")
            for k in range(B1):
                nc.tensor.matmul(
                    u2_bank[:], w2n_blocks[:, k, i, :], x1_bf[:, k, half], start=(k == 0), stop=(k == B1 - 1)
                )
            nc.scalar.copy(u2_dst, u2_bank[:])

        def project_t2(i, half, u2_src, t2_dst):
            c2_bank = psum.tile([P, BANK], F32, name="c2_bank", tag="bank")
            for k in range(B1):
                nc.tensor.matmul(
                    c2_bank[:], w2c_blocks[:, k, i, :], x1_bf[:, k, half], start=(k == 0), stop=(k == B1 - 1)
                )
            nc.vector.scalar_tensor_tensor(
                out=t2_dst, in0=c2_bank[:], scalar=b2_cols[:, i : i + 1], in1=u2_src, op0=ALU.add, op1=ALU.subtract
            )

        def half_rows(c):
            half = slice(c * BANK, (c + 1) * BANK)
            u2_halves = [halves.tile([P, BANK], F32, name="u2_half") for i in range(EARLY)]
            for i in range(EARLY):
                project_u2(i, half, u2_halves[i][:])
                nc.sync.dma_start(u2_rows[:, i, half], u2_halves[i][:])
            for i in range(EARLY):
                t2_half = halves.tile([P, BANK], F32, name="t2_half")
                project_t2(i, half, u2_halves[i][:], t2_half[:])
                nc.sync.dma_start(t2_rows[:, i, half], t2_half[:])

        half_rows(0)

        for g in range(EARLY // GROUP, B2 // GROUP):
            group = slice(g * GROUP, (g + 1) * GROUP)
            pieces = [(j, slice(c * BANK, (c + 1) * BANK)) for j in range(GROUP) for c in range(HALVES)]
            u2_sb = stage.tile([P, GROUP, NODES], F32, name="u2_sb")
            for j, half in pieces:
                project_u2(g * GROUP + j, half, u2_sb[:, j, half])
            nc.scalar.dma_start(u2_rows[:, group, :], u2_sb[:])
            t2_sb = stage.tile([P, GROUP, NODES], F32, name="t2_sb")
            for j, half in pieces:
                project_t2(g * GROUP + j, half, u2_sb[:, j, half], t2_sb[:, j, half])
            nc.sync.dma_start(t2_rows[:, group, :], t2_sb[:])
            if g == EARLY // GROUP:
                half_rows(1)
